import numpy as np
import ml_dtypes


def mxq(x, axis, fmt="e4m3"):
    dtype, down = {"e4m3": (ml_dtypes.float8_e4m3fn, 7), "e5m2": (ml_dtypes.float8_e5m2, 14)}[fmt]
    v = np.moveaxis(np.asarray(x, np.float32).astype(ml_dtypes.bfloat16).astype(np.float64), axis, -1)
    blocks = v.reshape(v.shape[:-1] + (-1, 32))
    amax = np.abs(blocks).max(-1, keepdims=True)
    byte = np.maximum(np.where(amax > 0, np.frexp(amax)[1] - 1 + 127, 0) - down, 1)
    scale = np.exp2(byte - 127.0)
    codes = (blocks / scale).astype(np.float32).astype(dtype).astype(np.float64)
    return np.moveaxis((codes * scale).reshape(v.shape), -1, axis)


WIDE = False


def mx_kscale(k):
    if not WIDE:
        return np.ones(k)
    levels = np.array([10, -10, 5, -5, 0])
    a = np.random.permutation(np.resize(levels, k // 512 * 4)).reshape(k // 512, 4)
    idx = np.arange(k)
    return np.exp2(a[idx // 512, idx % 128 // 32])


BF16 = ml_dtypes.bfloat16


def bf(x):
    return np.asarray(x, np.float32).astype(BF16)


def f64(x):
    return np.asarray(x).astype(np.float64)


B, T, N, C, WIN, F = 2, 6, 512, 512, 3, 2
NW = T - WIN + 1


def sigmoid(v):
    return 1.0 / (1.0 + np.exp(-v))


def setup_inputs():
    t = mx_kscale(C)
    return {"agg": bf(np.random.standard_normal((B, NW, N, C)) * t),
            "W": bf(np.random.standard_normal((NW, F, C, 2 * C)) / np.sqrt(C) / t[:, None]),
            "b": bf(np.random.standard_normal((NW, F, 2 * C)) * 0.3)}


def reference(agg, W, b):
    pre = (mxq(f64(agg), 3, "e4m3")[:, :, None] @ mxq(f64(W), 2, "e4m3")) + f64(b)[None, :, :, None, :]
    lhs, rhs = pre[..., :C], pre[..., C:]
    glu = lhs * sigmoid(rhs)
    return glu.max(axis=2)

@@ -1,0 +1,293 @@
+from contextlib import ExitStack
+
+import concourse.mybir as mybir
+from concourse.masks import make_identity
+
+F32 = mybir.dt.float32
+BF16 = mybir.dt.bfloat16
+U32 = mybir.dt.uint32
+U8 = mybir.dt.uint8
+FP8X4 = mybir.dt.float8_e4m3fn_x4
+ALU = mybir.AluOpType
+ACT = mybir.ActivationFunctionType
+
+P = 128
+FLOPS = 2 * 2 * 4 * 2 * 512 * 512 * 1024
+
+MANUAL = True
+CV = 576
+N_ROUNDS = 8
+
+
+def tile_stsindividuallayer_pb_t_kernel(tc, agg, W, b, out):
+    nc = tc.nc
+    with ExitStack() as ctx:
+        const = ctx.enter_context(tc.tile_pool(name="const", bufs=1))
+        rawp = ctx.enter_context(tc.tile_pool(name="raw", bufs=1))
+        wgp = ctx.enter_context(tc.tile_pool(name="wgp", bufs=2))
+        wqp = ctx.enter_context(tc.tile_pool(name="wqp", bufs=4))
+        agp = ctx.enter_context(tc.tile_pool(name="agp", bufs=2))
+        aqp = ctx.enter_context(tc.tile_pool(name="aqp", bufs=3))
+        sp = ctx.enter_context(tc.tile_pool(name="sp", bufs=4))
+        g0p = ctx.enter_context(tc.tile_pool(name="g0p", bufs=2))
+        g1p = ctx.enter_context(tc.tile_pool(name="g1p", bufs=3))
+        op = ctx.enter_context(tc.tile_pool(name="op", bufs=2))
+        psm = ctx.enter_context(tc.psum_pool(name="psm", bufs=6))
+        pst = ctx.enter_context(tc.psum_pool(name="pst", bufs=2))
+        if MANUAL:
+            ctx.enter_context(tc.manual_schedule())
+
+        araw = {}
+        wraw = {}
+        wgt = {}
+        wqt = {}
+        wst = {}
+        agt = {}
+        aqt = {}
+        ast = {}
+        xts = {}
+        rbs = {}
+        lbs = {}
+        sts = {}
+        g0t = {}
+        g1t = {}
+        obs = {}
+        ots = {}
+
+        def load_agg(r):
+            w, i = divmod(r, 2)
+            t = rawp.tile([P, 2048], BF16, name="araw%d" % r)
+            nc.sync.dma_start(out=t[:], in_=agg[i, w].rearrange("(p nt) k -> p (nt k)", nt=4))
+            araw[r] = t
+
+        def load_w(t_idx):
+            w, f = divmod(t_idx, 2)
+            t = rawp.tile([P, 4, 1024], BF16, name="wraw%d" % t_idx)
+            nc.sync.dma_start(
+                out=t[:].rearrange("q (u e) c -> q u (e c)", u=2),
+                in_=W[w, f].rearrange("(u q e) c -> q u (e c)", u=2, e=2),
+            )
+            wraw[t_idx] = t
+
+        braw = const.tile([P, P], BF16, name="braw")
+        nc.scalar.dma_start(out=braw[0:64, :], in_=b.rearrange("w f (j c) -> (w f j) c", c=P))
+        load_agg(0)
+        load_w(0)
+        load_w(1)
+        load_agg(1)
+        for w in range(1, 4):
+            load_w(2 * w)
+            load_agg(2 * w)
+            load_w(2 * w + 1)
+            load_agg(2 * w + 1)
+
+        ident = const.tile([P, P], F32, name="ident")
+        make_identity(nc, ident[:])
+        zero1 = const.tile([P, 1], F32, name="zero1")
+        nc.vector.memset(zero1[:], 0.0)
+        warm = const.tile([P, 1], F32, name="warm")
+        nc.scalar.activation(out=warm[:], in_=zero1[:], func=ACT.Sigmoid)
+        bf32 = const.tile([P, P], F32, name="bf32")
+        nc.vector.memset(bf32[:], 0.0)
+        nc.vector.tensor_copy(out=bf32[0:64, :], in_=braw[0:64, :])
+        bias_sb = const.tile([P, 64], F32, name="bias_sb")
+
+        def agg_t(r, h):
+            xt = pst.tile([P, 512], F32, name="xt", tag="tp")
+            words = araw[r][:].bitcast(F32)
+            for u in range(2):
+                for a in range(2):
+                    nt = 2 * h + a
+                    nc.tensor.transpose(
+                        xt[:, 256 * u + 128 * a : 256 * u + 128 * a + 128],
+                        words[:, 256 * nt + 128 * u : 256 * nt + 128 * u + 128],
+                        ident[:],
+                    )
+            xts[(r, h)] = xt
+
+        def agg_copy(r, h):
+            if h == 0:
+                agt[r] = agp.tile([P, 1024], F32, name="ag", tag="ag", align_bytes=64)
+            nc.scalar.copy(
+                out=agt[r][:, 512 * h : 512 * h + 512].rearrange("p (n u) -> p n u", u=2),
+                in_=xts[(r, h)][:].rearrange("p (u n) -> p n u", u=2),
+            )
+
+        def agg_q(r):
+            aqt[r] = aqp.tile([P, 512], U32, name="aq", tag="aq", align_bytes=64)
+            ast[r] = aqp.tile([P, 512], U8, name="asc", tag="asc", align_bytes=64)
+            nc.vector.quantize_mx(
+                out=aqt[r][:].bitcast(FP8X4), scales=ast[r][:], in_=agt[r][:].bitcast(BF16)
+            )
+
+        def regroup(t_idx, c0, c1, on_vector):
+            if t_idx not in wgt:
+                wgt[t_idx] = wgp.tile([P, 1024, 4], BF16, name="wg", tag="wg", align_bytes=64)
+            dst = wgt[t_idx][:, c0:c1, :].rearrange("p (c i) t -> p c t i", i=4)
+            src = wraw[t_idx][:, :, c0:c1].rearrange("p t (c i) -> p c t i", i=4)
+            if on_vector:
+                nc.vector.tensor_copy(out=dst, in_=src)
+            else:
+                nc.scalar.copy(out=dst, in_=src)
+
+        def w_q(t_idx):
+            wqt[t_idx] = wqp.tile([P, 1024], U32, name="wq", tag="wq", align_bytes=64)
+            wst[t_idx] = wqp.tile([P, 1024], U8, name="wsc", tag="wsc", align_bytes=64)
+            nc.vector.quantize_mx(
+                out=wqt[t_idx][:].bitcast(FP8X4),
+                scales=wst[t_idx][:],
+                in_=wgt[t_idx][:].rearrange("p c t -> p (c t)"),
+            )
+
+        def unit(uu):
+            r, u = divmod(uu, 8)
+            f, cb = divmod(u, 4)
+            return r, f, cb, 2 * (r // 2) + f
+
+        def one_pass(acc, t_idx, j, r):
+            nc.tensor.matmul_mx(
+                out=acc[:],
+                lhsT=wqt[t_idx][:, 128 * j : 128 * j + 128].bitcast(FP8X4),
+                lhsT_scale=wst[t_idx][:, 128 * j : 128 * j + 128],
+                rhs=aqt[r][:].bitcast(FP8X4),
+                rhs_scale=ast[r][:],
+                start=True,
+                stop=True,
+            )
+
+        def mx(uu):
+            r, f, cb, t_idx = unit(uu)
+            rbs[uu] = psm.tile([P, 512], F32, name="rb", tag="mx")
+            one_pass(rbs[uu], t_idx, 4 + cb, r)
+            lbs[uu] = psm.tile([P, 512], F32, name="lb", tag="mx")
+            one_pass(lbs[uu], t_idx, cb, r)
+
+        def sig(uu):
+            r, f, cb, t_idx = unit(uu)
+            col = 8 * t_idx + 4 + cb
+            sts[uu] = sp.tile([P, 512], F32, name="s", tag="s")
+            nc.scalar.activation(
+                out=sts[uu][:], in_=rbs[uu][:], func=ACT.Sigmoid, bias=bias_sb[:, col : col + 1], scale=1.0
+            )
+
+        def stt(uu):
+            r, f, cb, t_idx = unit(uu)
+            col = 8 * t_idx + cb
+            if f == 0:
+                if cb == 0:
+                    g0t[r] = g0p.tile([P, 4, 512], F32, name="g0", tag="g0")
+                dst = g0t[r][:, cb, :]
+            else:
+                g1t[(r, cb)] = g1p.tile([P, 512], F32, name="g1", tag="g1")
+                dst = g1t[(r, cb)][:]
+            nc.vector.scalar_tensor_tensor(
+                out=dst,
+                in0=lbs[uu][:],
+                scalar=bias_sb[:, col : col + 1],
+                in1=sts[uu][:],
+                op0=ALU.add,
+                op1=ALU.mult,
+            )
+
+        def vmax(r, cb):
+            nc.vector.tensor_tensor(
+                out=g0t[r][:, cb, :], in0=g0t[r][:, cb, :], in1=g1t[(r, cb)][:], op=ALU.max
+            )
+
+        def out_t(r, nt, big):
+            if big:
+                ob = psm.tile([P, 512], F32, name="ob2", tag="mx")
+            else:
+                ob = pst.tile([P, 512], F32, name="ob", tag="tp")
+            for cb in range(4):
+                nc.tensor.transpose(
+                    ob[:, 128 * cb : 128 * cb + 128], g0t[r][:, cb, 128 * nt : 128 * nt + 128], ident[:]
+                )
+            obs[(r, nt)] = ob
+
+        def out_copy(r, nt, on_vector):
+            if nt == 0:
+                ots[r] = op.tile([P, 4, 512], F32, name="o", tag="o")
+            if on_vector:
+                nc.vector.tensor_copy(out=ots[r][:, nt, :], in_=obs[(r, nt)][:])
+            else:
+                nc.scalar.copy(out=ots[r][:, nt, :], in_=obs[(r, nt)][:])
+
+        def store(r, n0, n1):
+            w, i = divmod(r, 2)
+            nc.sync.dma_start(
+                out=out[i, w].rearrange("(p nt) c -> p nt c", nt=4)[:, n0:n1, :], in_=ots[r][:, n0:n1, :]
+            )
+
+        hv = CV // 2
+        hs = (1024 - CV) // 2
+
+        agg_t(0, 0)
+        agg_t(0, 1)
+        bt = psm.tile([P, 512], F32, name="bt", tag="mx")
+        nc.tensor.transpose(bt[:, 0:128], bf32[:], ident[:])
+        nc.vector.tensor_copy(out=bias_sb[:], in_=bt[:, 0:64])
+        agg_copy(0, 0)
+        agg_copy(0, 1)
+        regroup(0, 0, CV, True)
+        regroup(0, CV, 1024, False)
+        agg_q(0)
+        w_q(0)
+        regroup(1, 0, CV, True)
+        regroup(1, CV, 1024, False)
+        mx(0)
+        mx(1)
+
+        for r in range(N_ROUNDS):
+            for u in range(8):
+                uu = 8 * r + u
+                if uu + 2 < 8 * N_ROUNDS:
+                    mx(uu + 2)
+                if u == 0 and r + 1 < N_ROUNDS:
+                    agg_t(r + 1, 0)
+                    agg_t(r + 1, 1)
+                if r >= 1:
+                    if u == 3:
+                        out_t(r - 1, 0, False)
+                        out_t(r - 1, 1, False)
+                    if u == 5:
+                        out_t(r - 1, 2, False)
+                    if u == 6:
+                        out_t(r - 1, 3, False)
+                sig(uu)
+                if u == 0 and r + 2 < 8:
+                    regroup(r + 2, CV, CV + hs, False)
+                if u in (1, 2) and r + 1 < N_ROUNDS:
+                    agg_copy(r + 1, u - 1)
+                if u == 3 and r + 2 < 8:
+                    regroup(r + 2, CV + hs, 1024, False)
+                if u >= 4 and r >= 1:
+                    out_copy(r - 1, u - 4, False)
+                    if u == 7:
+                        store(r - 1, 0, 4)
+                stt(uu)
+                if u == 0 and r + 1 < 8:
+                    w_q(r + 1)
+                if u == 1 and r >= 1:
+                    vmax(r - 1, 3)
+                if u == 2 and r + 2 < 8:
+                    regroup(r + 2, 0, hv, True)
+                if u == 3 and r + 2 < 8:
+                    regroup(r + 2, hv, CV, True)
+                if u == 4 and r + 1 < N_ROUNDS:
+                    agg_q(r + 1)
+                if u >= 5:
+                    vmax(r, u - 5)
+
+        last = N_ROUNDS - 1
+        vmax(last, 3)
+        out_t(last, 0, False)
+        out_t(last, 1, False)
+        out_t(last, 2, True)
+        out_t(last, 3, True)
+        out_copy(last, 0, False)
+        out_copy(last, 1, True)
+        store(last, 0, 2)
+        out_copy(last, 2, False)
+        out_copy(last, 3, True)
+        store(last, 2, 4)

@@ -71,8 +71,19 @@ def tile_stsindividuallayer_pb_t_kernel(tc, agg, W, b, out):
 
         braw = const.tile([P, P], BF16, name="braw")
         nc.scalar.dma_start(out=braw[0:64, :], in_=b.rearrange("w f (j c) -> (w f j) c", c=P))
+        w0 = rawp.tile([P, 4, 1024], BF16, name="wraw0")
+        wraw[0] = w0
+
+        def load_w0_half(c0):
+            for u in range(2):
+                nc.sync.dma_start(
+                    out=w0[:, 2 * u : 2 * u + 2, c0 : c0 + 512],
+                    in_=W[0, 0][256 * u : 256 * u + 256, c0 : c0 + 512].rearrange("(q e) c -> q e c", e=2),
+                )
+
+        load_w0_half(512)
         load_agg(0)
-        load_w(0)
+        load_w0_half(0)
         load_w(1)
         load_agg(1)
         for w in range(1, 4):
@@ -105,13 +116,15 @@ def tile_stsindividuallayer_pb_t_kernel(tc, agg, W, b, out):
                     )
             xts[(r, h)] = xt
 
-        def agg_copy(r, h):
+        def agg_copy(r, h, on_vector=False):
             if h == 0:
                 agt[r] = agp.tile([P, 1024], F32, name="ag", tag="ag", align_bytes=64)
-            nc.scalar.copy(
-                out=agt[r][:, 512 * h : 512 * h + 512].rearrange("p (n u) -> p n u", u=2),
-                in_=xts[(r, h)][:].rearrange("p (u n) -> p n u", u=2),
-            )
+            dst = agt[r][:, 512 * h : 512 * h + 512].rearrange("p (n u) -> p n u", u=2)
+            src = xts[(r, h)][:].rearrange("p (u n) -> p n u", u=2)
+            if on_vector:
+                nc.vector.tensor_copy(out=dst, in_=src)
+            else:
+                nc.scalar.copy(out=dst, in_=src)
 
         def agg_q(r):
             aqt[r] = aqp.tile([P, 512], U32, name="aq", tag="aq", align_bytes=64)
@@ -130,13 +143,14 @@ def tile_stsindividuallayer_pb_t_kernel(tc, agg, W, b, out):
             else:
                 nc.scalar.copy(out=dst, in_=src)
 
-        def w_q(t_idx):
-            wqt[t_idx] = wqp.tile([P, 1024], U32, name="wq", tag="wq", align_bytes=64)
-            wst[t_idx] = wqp.tile([P, 1024], U8, name="wsc", tag="wsc", align_bytes=64)
+        def w_q(t_idx, c0=0, c1=1024):
+            if t_idx not in wqt:
+                wqt[t_idx] = wqp.tile([P, 1024], U32, name="wq", tag="wq", align_bytes=64)
+                wst[t_idx] = wqp.tile([P, 1024], U8, name="wsc", tag="wsc", align_bytes=64)
             nc.vector.quantize_mx(
-                out=wqt[t_idx][:].bitcast(FP8X4),
-                scales=wst[t_idx][:],
-                in_=wgt[t_idx][:].rearrange("p c t -> p (c t)"),
+                out=wqt[t_idx][:, c0:c1].bitcast(FP8X4),
+                scales=wst[t_idx][:, c0:c1],
+                in_=wgt[t_idx][:, c0:c1, :].rearrange("p c t -> p (c t)"),
             )
 
         def unit(uu):
@@ -155,12 +169,19 @@ def tile_stsindividuallayer_pb_t_kernel(tc, agg, W, b, out):
                 stop=True,
             )
 
-        def mx(uu):
+        def mx_r(uu):
             r, f, cb, t_idx = unit(uu)
             rbs[uu] = psm.tile([P, 512], F32, name="rb", tag="mx")
             one_pass(rbs[uu], t_idx, 4 + cb, r)
+
+        def mx_l(uu):
+            r, f, cb, t_idx = unit(uu)
             lbs[uu] = psm.tile([P, 512], F32, name="lb", tag="mx")
             one_pass(lbs[uu], t_idx, cb, r)
+
+        def mx(uu):
+            mx_r(uu)
+            mx_l(uu)
 
         def sig(uu):
             r, f, cb, t_idx = unit(uu)
@@ -194,16 +215,21 @@ def tile_stsindividuallayer_pb_t_kernel(tc, agg, W, b, out):
                 out=g0t[r][:, cb, :], in0=g0t[r][:, cb, :], in1=g1t[(r, cb)][:], op=ALU.max
             )
 
-        def out_t(r, nt, big):
+        def out_bank(r, nt, big):
             if big:
-                ob = psm.tile([P, 512], F32, name="ob2", tag="mx")
+                obs[(r, nt)] = psm.tile([P, 512], F32, name="ob2", tag="mx")
             else:
-                ob = pst.tile([P, 512], F32, name="ob", tag="tp")
+                obs[(r, nt)] = pst.tile([P, 512], F32, name="ob", tag="tp")
+
+        def out_t1(r, nt, cb):
+            nc.tensor.transpose(
+                obs[(r, nt)][:, 128 * cb : 128 * cb + 128], g0t[r][:, cb, 128 * nt : 128 * nt + 128], ident[:]
+            )
+
+        def out_t(r, nt):
+            out_bank(r, nt, False)
             for cb in range(4):
-                nc.tensor.transpose(
-                    ob[:, 128 * cb : 128 * cb + 128], g0t[r][:, cb, 128 * nt : 128 * nt + 128], ident[:]
-                )
-            obs[(r, nt)] = ob
+                out_t1(r, nt, cb)
 
         def out_copy(r, nt, on_vector):
             if nt == 0:
@@ -222,72 +248,142 @@ def tile_stsindividuallayer_pb_t_kernel(tc, agg, W, b, out):
         hv = CV // 2
         hs = (1024 - CV) // 2
 
+        VR = 336
         agg_t(0, 0)
         agg_t(0, 1)
         bt = psm.tile([P, 512], F32, name="bt", tag="mx")
         nc.tensor.transpose(bt[:, 0:128], bf32[:], ident[:])
+        regroup(0, 512 + VR, 1024, False)
+        agg_copy(0, 0, False)
+        regroup(0, VR, 512, False)
+        regroup(0, 512, 512 + VR, True)
+        w_q(0, 512, 1024)
         nc.vector.tensor_copy(out=bias_sb[:], in_=bt[:, 0:64])
-        agg_copy(0, 0)
-        agg_copy(0, 1)
-        regroup(0, 0, CV, True)
-        regroup(0, CV, 1024, False)
+        agg_copy(0, 1, True)
         agg_q(0)
-        w_q(0)
-        regroup(1, 0, CV, True)
-        regroup(1, CV, 1024, False)
-        mx(0)
-        mx(1)
+        regroup(0, 0, VR, True)
+        w_q(0, 0, 512)
+        for uu in range(3):
+            mx_r(uu)
+        for uu in range(3):
+            mx_l(uu)
+
+        def rg_s(t_idx, k):
+            regroup(t_idx, CV + hs * k, CV + hs * (k + 1), False)
+
+        def rg_v(t_idx, k):
+            regroup(t_idx, hv * k, hv * (k + 1), True)
 
         for r in range(N_ROUNDS):
             for u in range(8):
                 uu = 8 * r + u
-                if uu + 2 < 8 * N_ROUNDS:
-                    mx(uu + 2)
-                if u == 0 and r + 1 < N_ROUNDS:
-                    agg_t(r + 1, 0)
-                    agg_t(r + 1, 1)
-                if r >= 1:
+                if r == 0:
+                    if u == 1:
+                        agg_t(1, 0)
+                        agg_t(1, 1)
+                    if u == 2:
+                        mx(3)
                     if u == 3:
-                        out_t(r - 1, 0, False)
-                        out_t(r - 1, 1, False)
+                        mx(4)
+                        mx(5)
+                    if u > 3:
+                        mx(uu + 2)
+                elif uu + 2 < 8 * N_ROUNDS:
+                    mx(uu + 2)
+                if 1 <= r < 7:
+                    if u == 0:
+                        agg_t(r + 1, 0)
+                        agg_t(r + 1, 1)
+                    if u == 3:
+                        out_t(r - 1, 0)
+                        out_t(r - 1, 1)
                     if u == 5:
-                        out_t(r - 1, 2, False)
+                        out_t(r - 1, 2)
                     if u == 6:
-                        out_t(r - 1, 3, False)
-                sig(uu)
-                if u == 0 and r + 2 < 8:
-                    regroup(r + 2, CV, CV + hs, False)
-                if u in (1, 2) and r + 1 < N_ROUNDS:
-                    agg_copy(r + 1, u - 1)
-                if u == 3 and r + 2 < 8:
-                    regroup(r + 2, CV + hs, 1024, False)
-                if u >= 4 and r >= 1:
-                    out_copy(r - 1, u - 4, False)
+                        out_t(r - 1, 3)
+                if r == 7:
+                    if u == 1:
+                        out_t(6, 0)
+                        out_t(6, 1)
+                    if u == 3:
+                        out_t(6, 2)
+                    if u == 4:
+                        out_t(6, 3)
+                    if u == 6:
+                        out_bank(7, 0, False)
+                        out_bank(7, 1, False)
+                        out_t1(7, 0, 0)
+                        out_t1(7, 1, 0)
                     if u == 7:
-                        store(r - 1, 0, 4)
+                        out_bank(7, 2, True)
+                        out_bank(7, 3, True)
+                        out_t1(7, 2, 0)
+                        out_t1(7, 3, 0)
+                        for nt in range(4):
+                            out_t1(7, nt, 1)
+                sig(uu)
+                if r == 0:
+                    if u in (0, 1):
+                        rg_s(1, u)
+                    if u in (2, 3):
+                        agg_copy(1, u - 2)
+                    if u in (4, 5):
+                        rg_s(2, u - 4)
+                elif r < 7:
+                    if u == 0 and r + 2 < 8:
+                        rg_s(r + 2, 0)
+                    if u in (1, 2):
+                        agg_copy(r + 1, u - 1)
+                    if u == 3 and r + 2 < 8:
+                        rg_s(r + 2, 1)
+                    if u >= 4:
+                        out_copy(r - 1, u - 4, False)
+                        if u == 7:
+                            store(r - 1, 0, 4)
+                else:
+                    if 2 <= u <= 5:
+                        out_copy(6, u - 2, False)
+                        if u == 5:
+                            store(6, 0, 4)
                 stt(uu)
-                if u == 0 and r + 1 < 8:
-                    w_q(r + 1)
-                if u == 1 and r >= 1:
-                    vmax(r - 1, 3)
-                if u == 2 and r + 2 < 8:
-                    regroup(r + 2, 0, hv, True)
-                if u == 3 and r + 2 < 8:
-                    regroup(r + 2, hv, CV, True)
-                if u == 4 and r + 1 < N_ROUNDS:
-                    agg_q(r + 1)
-                if u >= 5:
-                    vmax(r, u - 5)
+                if r == 0:
+                    if u in (0, 1):
+                        rg_v(1, u)
+                    if u == 2:
+                        w_q(1)
+                    if u == 3:
+                        rg_v(2, 0)
+                    if u == 4:
+                        agg_q(1)
+                    if u == 6:
+                        rg_v(2, 1)
+                    if u >= 5:
+                        vmax(0, u - 5)
+                elif r < 7:
+                    if u == 0:
+                        w_q(r + 1)
+                    if u == 1:
+                        vmax(r - 1, 3)
+                    if u in (2, 3) and r + 2 < 8:
+                        rg_v(r + 2, u - 2)
+                    if u == 4:
+                        agg_q(r + 1)
+                    if u >= 5:
+                        vmax(r, u - 5)
+                else:
+                    if u == 0:
+                        vmax(6, 3)
+                    if u >= 5:
+                        vmax(7, u - 5)
 
-        last = N_ROUNDS - 1
-        vmax(last, 3)
-        out_t(last, 0, False)
-        out_t(last, 1, False)
-        out_t(last, 2, True)
-        out_t(last, 3, True)
-        out_copy(last, 0, False)
-        out_copy(last, 1, True)
-        store(last, 0, 2)
-        out_copy(last, 2, False)
-        out_copy(last, 3, True)
-        store(last, 2, 4)
+        for nt in range(4):
+            out_t1(7, nt, 2)
+        vmax(7, 3)
+        for nt in range(4):
+            out_t1(7, nt, 3)
+        out_copy(7, 0, False)
+        out_copy(7, 1, True)
+        store(7, 0, 2)
+        out_copy(7, 2, False)
+        out_copy(7, 3, True)
+        store(7, 2, 4)

@@ -14,7 +14,7 @@ ACT = mybir.ActivationFunctionType
 P = 128
 FLOPS = 2 * 2 * 4 * 2 * 512 * 512 * 1024
 
-MANUAL = True
+MANUAL = False
 CV = 576
 N_ROUNDS = 8
 
@@ -71,19 +71,8 @@ def tile_stsindividuallayer_pb_t_kernel(tc, agg, W, b, out):
 
         braw = const.tile([P, P], BF16, name="braw")
         nc.scalar.dma_start(out=braw[0:64, :], in_=b.rearrange("w f (j c) -> (w f j) c", c=P))
-        w0 = rawp.tile([P, 4, 1024], BF16, name="wraw0")
-        wraw[0] = w0
-
-        def load_w0_half(c0):
-            for u in range(2):
-                nc.sync.dma_start(
-                    out=w0[:, 2 * u : 2 * u + 2, c0 : c0 + 512],
-                    in_=W[0, 0][256 * u : 256 * u + 256, c0 : c0 + 512].rearrange("(q e) c -> q e c", e=2),
-                )
-
-        load_w0_half(512)
         load_agg(0)
-        load_w0_half(0)
+        load_w(0)
         load_w(1)
         load_agg(1)
         for w in range(1, 4):
@@ -116,15 +105,13 @@ def tile_stsindividuallayer_pb_t_kernel(tc, agg, W, b, out):
                     )
             xts[(r, h)] = xt
 
-        def agg_copy(r, h, on_vector=False):
+        def agg_copy(r, h):
             if h == 0:
                 agt[r] = agp.tile([P, 1024], F32, name="ag", tag="ag", align_bytes=64)
-            dst = agt[r][:, 512 * h : 512 * h + 512].rearrange("p (n u) -> p n u", u=2)
-            src = xts[(r, h)][:].rearrange("p (u n) -> p n u", u=2)
-            if on_vector:
-                nc.vector.tensor_copy(out=dst, in_=src)
-            else:
-                nc.scalar.copy(out=dst, in_=src)
+            nc.scalar.copy(
+                out=agt[r][:, 512 * h : 512 * h + 512].rearrange("p (n u) -> p n u", u=2),
+                in_=xts[(r, h)][:].rearrange("p (u n) -> p n u", u=2),
+            )
 
         def agg_q(r):
             aqt[r] = aqp.tile([P, 512], U32, name="aq", tag="aq", align_bytes=64)
@@ -143,14 +130,13 @@ def tile_stsindividuallayer_pb_t_kernel(tc, agg, W, b, out):
             else:
                 nc.scalar.copy(out=dst, in_=src)
 
-        def w_q(t_idx, c0=0, c1=1024):
-            if t_idx not in wqt:
-                wqt[t_idx] = wqp.tile([P, 1024], U32, name="wq", tag="wq", align_bytes=64)
-                wst[t_idx] = wqp.tile([P, 1024], U8, name="wsc", tag="wsc", align_bytes=64)
+        def w_q(t_idx):
+            wqt[t_idx] = wqp.tile([P, 1024], U32, name="wq", tag="wq", align_bytes=64)
+            wst[t_idx] = wqp.tile([P, 1024], U8, name="wsc", tag="wsc", align_bytes=64)
             nc.vector.quantize_mx(
-                out=wqt[t_idx][:, c0:c1].bitcast(FP8X4),
-                scales=wst[t_idx][:, c0:c1],
-                in_=wgt[t_idx][:, c0:c1, :].rearrange("p c t -> p (c t)"),
+                out=wqt[t_idx][:].bitcast(FP8X4),
+                scales=wst[t_idx][:],
+                in_=wgt[t_idx][:].rearrange("p c t -> p (c t)"),
             )
 
         def unit(uu):
@@ -169,19 +155,12 @@ def tile_stsindividuallayer_pb_t_kernel(tc, agg, W, b, out):
                 stop=True,
             )
 
-        def mx_r(uu):
+        def mx(uu):
             r, f, cb, t_idx = unit(uu)
             rbs[uu] = psm.tile([P, 512], F32, name="rb", tag="mx")
             one_pass(rbs[uu], t_idx, 4 + cb, r)
-
-        def mx_l(uu):
-            r, f, cb, t_idx = unit(uu)
             lbs[uu] = psm.tile([P, 512], F32, name="lb", tag="mx")
             one_pass(lbs[uu], t_idx, cb, r)
-
-        def mx(uu):
-            mx_r(uu)
-            mx_l(uu)
 
         def sig(uu):
             r, f, cb, t_idx = unit(uu)
@@ -215,21 +194,16 @@ def tile_stsindividuallayer_pb_t_kernel(tc, agg, W, b, out):
                 out=g0t[r][:, cb, :], in0=g0t[r][:, cb, :], in1=g1t[(r, cb)][:], op=ALU.max
             )
 
-        def out_bank(r, nt, big):
+        def out_t(r, nt, big):
             if big:
-                obs[(r, nt)] = psm.tile([P, 512], F32, name="ob2", tag="mx")
+                ob = psm.tile([P, 512], F32, name="ob2", tag="mx")
             else:
-                obs[(r, nt)] = pst.tile([P, 512], F32, name="ob", tag="tp")
-
-        def out_t1(r, nt, cb):
-            nc.tensor.transpose(
-                obs[(r, nt)][:, 128 * cb : 128 * cb + 128], g0t[r][:, cb, 128 * nt : 128 * nt + 128], ident[:]
-            )
-
-        def out_t(r, nt):
-            out_bank(r, nt, False)
+                ob = pst.tile([P, 512], F32, name="ob", tag="tp")
             for cb in range(4):
-                out_t1(r, nt, cb)
+                nc.tensor.transpose(
+                    ob[:, 128 * cb : 128 * cb + 128], g0t[r][:, cb, 128 * nt : 128 * nt + 128], ident[:]
+                )
+            obs[(r, nt)] = ob
 
         def out_copy(r, nt, on_vector):
             if nt == 0:
@@ -248,142 +222,72 @@ def tile_stsindividuallayer_pb_t_kernel(tc, agg, W, b, out):
         hv = CV // 2
         hs = (1024 - CV) // 2
 
-        VR = 336
         agg_t(0, 0)
         agg_t(0, 1)
         bt = psm.tile([P, 512], F32, name="bt", tag="mx")
         nc.tensor.transpose(bt[:, 0:128], bf32[:], ident[:])
-        regroup(0, 512 + VR, 1024, False)
-        agg_copy(0, 0, False)
-        regroup(0, VR, 512, False)
-        regroup(0, 512, 512 + VR, True)
-        w_q(0, 512, 1024)
         nc.vector.tensor_copy(out=bias_sb[:], in_=bt[:, 0:64])
-        agg_copy(0, 1, True)
+        agg_copy(0, 0)
+        agg_copy(0, 1)
+        regroup(0, 0, CV, True)
+        regroup(0, CV, 1024, False)
         agg_q(0)
-        regroup(0, 0, VR, True)
-        w_q(0, 0, 512)
-        for uu in range(3):
-            mx_r(uu)
-        for uu in range(3):
-            mx_l(uu)
-
-        def rg_s(t_idx, k):
-            regroup(t_idx, CV + hs * k, CV + hs * (k + 1), False)
-
-        def rg_v(t_idx, k):
-            regroup(t_idx, hv * k, hv * (k + 1), True)
+        w_q(0)
+        regroup(1, 0, CV, True)
+        regroup(1, CV, 1024, False)
+        mx(0)
+        mx(1)
 
         for r in range(N_ROUNDS):
             for u in range(8):
                 uu = 8 * r + u
-                if r == 0:
-                    if u == 1:
-                        agg_t(1, 0)
-                        agg_t(1, 1)
-                    if u == 2:
-                        mx(3)
-                    if u == 3:
-                        mx(4)
-                        mx(5)
-                    if u > 3:
-                        mx(uu + 2)
-                elif uu + 2 < 8 * N_ROUNDS:
+                if uu + 2 < 8 * N_ROUNDS:
                     mx(uu + 2)
-                if 1 <= r < 7:
-                    if u == 0:
-                        agg_t(r + 1, 0)
-                        agg_t(r + 1, 1)
+                if u == 0 and r + 1 < N_ROUNDS:
+                    agg_t(r + 1, 0)
+                    agg_t(r + 1, 1)
+                if r >= 1:
                     if u == 3:
-                        out_t(r - 1, 0)
-                        out_t(r - 1, 1)
+                        out_t(r - 1, 0, False)
+                        out_t(r - 1, 1, False)
                     if u == 5:
-                        out_t(r - 1, 2)
+                        out_t(r - 1, 2, False)
                     if u == 6:
-                        out_t(r - 1, 3)
-                if r == 7:
-                    if u == 1:
-                        out_t(6, 0)
-                        out_t(6, 1)
-                    if u == 3:
-                        out_t(6, 2)
-                    if u == 4:
-                        out_t(6, 3)
-                    if u == 6:
-                        out_bank(7, 0, False)
-                        out_bank(7, 1, False)
-                        out_t1(7, 0, 0)
-                        out_t1(7, 1, 0)
-                    if u == 7:
-                        out_bank(7, 2, True)
-                        out_bank(7, 3, True)
-                        out_t1(7, 2, 0)
-                        out_t1(7, 3, 0)
-                        for nt in range(4):
-                            out_t1(7, nt, 1)
+                        out_t(r - 1, 3, False)
                 sig(uu)
-                if r == 0:
-                    if u in (0, 1):
-                        rg_s(1, u)
-                    if u in (2, 3):
-                        agg_copy(1, u - 2)
-                    if u in (4, 5):
-                        rg_s(2, u - 4)
-                elif r < 7:
-                    if u == 0 and r + 2 < 8:
-                        rg_s(r + 2, 0)
-                    if u in (1, 2):
-                        agg_copy(r + 1, u - 1)
-                    if u == 3 and r + 2 < 8:
-                        rg_s(r + 2, 1)
-                    if u >= 4:
-                        out_copy(r - 1, u - 4, False)
-                        if u == 7:
-                            store(r - 1, 0, 4)
-                else:
-                    if 2 <= u <= 5:
-                        out_copy(6, u - 2, False)
-                        if u == 5:
-                            store(6, 0, 4)
+                if u == 0 and r + 2 < 8:
+                    regroup(r + 2, CV, CV + hs, False)
+                if u in (1, 2) and r + 1 < N_ROUNDS:
+                    agg_copy(r + 1, u - 1)
+                if u == 3 and r + 2 < 8:
+                    regroup(r + 2, CV + hs, 1024, False)
+                if u >= 4 and r >= 1:
+                    out_copy(r - 1, u - 4, False)
+                    if u == 7:
+                        store(r - 1, 0, 4)
                 stt(uu)
-                if r == 0:
-                    if u in (0, 1):
-                        rg_v(1, u)
-                    if u == 2:
-                        w_q(1)
-                    if u == 3:
-                        rg_v(2, 0)
-                    if u == 4:
-                        agg_q(1)
-                    if u == 6:
-                        rg_v(2, 1)
-                    if u >= 5:
-                        vmax(0, u - 5)
-                elif r < 7:
-                    if u == 0:
-                        w_q(r + 1)
-                    if u == 1:
-                        vmax(r - 1, 3)
-                    if u in (2, 3) and r + 2 < 8:
-                        rg_v(r + 2, u - 2)
-                    if u == 4:
-                        agg_q(r + 1)
-                    if u >= 5:
-                        vmax(r, u - 5)
-                else:
-                    if u == 0:
-                        vmax(6, 3)
-                    if u >= 5:
-                        vmax(7, u - 5)
+                if u == 0 and r + 1 < 8:
+                    w_q(r + 1)
+                if u == 1 and r >= 1:
+                    vmax(r - 1, 3)
+                if u == 2 and r + 2 < 8:
+                    regroup(r + 2, 0, hv, True)
+                if u == 3 and r + 2 < 8:
+                    regroup(r + 2, hv, CV, True)
+                if u == 4 and r + 1 < N_ROUNDS:
+                    agg_q(r + 1)
+                if u >= 5:
+                    vmax(r, u - 5)
 
-        for nt in range(4):
-            out_t1(7, nt, 2)
-        vmax(7, 3)
-        for nt in range(4):
-            out_t1(7, nt, 3)
-        out_copy(7, 0, False)
-        out_copy(7, 1, True)
-        store(7, 0, 2)
-        out_copy(7, 2, False)
-        out_copy(7, 3, True)
-        store(7, 2, 4)
+        last = N_ROUNDS - 1
+        vmax(last, 3)
+        out_t(last, 0, False)
+        out_t(last, 1, False)
+        out_t(last, 2, True)
+        out_t(last, 3, True)
+        out_copy(last, 0, False)
+        out_copy(last, 1, True)
+        store(last, 0, 2)
+        out_copy(last, 2, False)
+        out_copy(last, 3, True)
+        store(last, 2, 4)

@@ -24,14 +24,14 @@ def tile_stsindividuallayer_pb_t_kernel(tc, agg, W, b, out):
     with ExitStack() as ctx:
         const = ctx.enter_context(tc.tile_pool(name="const", bufs=1))
         rawp = ctx.enter_context(tc.tile_pool(name="raw", bufs=1))
-        wgp = ctx.enter_context(tc.tile_pool(name="wgp", bufs=2))
+        wgp = ctx.enter_context(tc.tile_pool(name="wgp", bufs=3))
         wqp = ctx.enter_context(tc.tile_pool(name="wqp", bufs=4))
-        agp = ctx.enter_context(tc.tile_pool(name="agp", bufs=2))
-        aqp = ctx.enter_context(tc.tile_pool(name="aqp", bufs=3))
-        sp = ctx.enter_context(tc.tile_pool(name="sp", bufs=4))
+        agp = ctx.enter_context(tc.tile_pool(name="agp", bufs=3))
+        aqp = ctx.enter_context(tc.tile_pool(name="aqp", bufs=4))
+        sp = ctx.enter_context(tc.tile_pool(name="sp", bufs=6))
         g0p = ctx.enter_context(tc.tile_pool(name="g0p", bufs=2))
-        g1p = ctx.enter_context(tc.tile_pool(name="g1p", bufs=3))
-        op = ctx.enter_context(tc.tile_pool(name="op", bufs=2))
+        g1p = ctx.enter_context(tc.tile_pool(name="g1p", bufs=4))
+        op = ctx.enter_context(tc.tile_pool(name="op", bufs=3))
         psm = ctx.enter_context(tc.psum_pool(name="psm", bufs=6))
         pst = ctx.enter_context(tc.psum_pool(name="pst", bufs=2))
         if MANUAL:
@@ -157,10 +157,10 @@ def tile_stsindividuallayer_pb_t_kernel(tc, agg, W, b, out):
 
         def mx(uu):
             r, f, cb, t_idx = unit(uu)
-            rbs[uu] = psm.tile([P, 512], F32, name="rb", tag="mx")
-            one_pass(rbs[uu], t_idx, 4 + cb, r)
             lbs[uu] = psm.tile([P, 512], F32, name="lb", tag="mx")
             one_pass(lbs[uu], t_idx, cb, r)
+            rbs[uu] = psm.tile([P, 512], F32, name="rb", tag="mx")
+            one_pass(rbs[uu], t_idx, 4 + cb, r)
 
         def sig(uu):
             r, f, cb, t_idx = unit(uu)

from contextlib import ExitStack

import concourse.mybir as mybir
from concourse.masks import make_identity

F32 = mybir.dt.float32
BF16 = mybir.dt.bfloat16
U32 = mybir.dt.uint32
U8 = mybir.dt.uint8
FP8X4 = mybir.dt.float8_e4m3fn_x4
ALU = mybir.AluOpType
ACT = mybir.ActivationFunctionType

P = 128
FLOPS = 2 * 2 * 4 * 2 * 512 * 512 * 1024

MANUAL = False
CV = 576
N_ROUNDS = 8


def tile_stsindividuallayer_pb_t_kernel(tc, agg, W, b, out):
    nc = tc.nc
    with ExitStack() as ctx:
        const = ctx.enter_context(tc.tile_pool(name="const", bufs=1))
        rawp = ctx.enter_context(tc.tile_pool(name="raw", bufs=1))
        wgp = ctx.enter_context(tc.tile_pool(name="wgp", bufs=3))
        wqp = ctx.enter_context(tc.tile_pool(name="wqp", bufs=4))
        agp = ctx.enter_context(tc.tile_pool(name="agp", bufs=3))
        aqp = ctx.enter_context(tc.tile_pool(name="aqp", bufs=4))
        sp = ctx.enter_context(tc.tile_pool(name="sp", bufs=6))
        g0p = ctx.enter_context(tc.tile_pool(name="g0p", bufs=2))
        g1p = ctx.enter_context(tc.tile_pool(name="g1p", bufs=4))
        op = ctx.enter_context(tc.tile_pool(name="op", bufs=3))
        psm = ctx.enter_context(tc.psum_pool(name="psm", bufs=6))
        pst = ctx.enter_context(tc.psum_pool(name="pst", bufs=2))
        if MANUAL:
            ctx.enter_context(tc.manual_schedule())

        araw = {}
        wraw = {}
        wgt = {}
        wqt = {}
        wst = {}
        agt = {}
        aqt = {}
        ast = {}
        xts = {}
        rbs = {}
        lbs = {}
        sts = {}
        g0t = {}
        g1t = {}
        obs = {}
        ots = {}

        def load_agg(r):
            w, i = divmod(r, 2)
            t = rawp.tile([P, 2048], BF16, name="araw%d" % r)
            nc.sync.dma_start(out=t[:], in_=agg[i, w].rearrange("(p nt) k -> p (nt k)", nt=4))
            araw[r] = t

        def load_w(t_idx):
            w, f = divmod(t_idx, 2)
            t = rawp.tile([P, 4, 1024], BF16, name="wraw%d" % t_idx)
            nc.sync.dma_start(
                out=t[:].rearrange("q (u e) c -> q u (e c)", u=2),
                in_=W[w, f].rearrange("(u q e) c -> q u (e c)", u=2, e=2),
            )
            wraw[t_idx] = t

        braw = const.tile([P, P], BF16, name="braw")
        nc.scalar.dma_start(out=braw[0:64, :], in_=b.rearrange("w f (j c) -> (w f j) c", c=P))
        load_agg(0)
        load_w(0)
        load_w(1)
        load_agg(1)
        for w in range(1, 4):
            load_w(2 * w)
            load_agg(2 * w)
            load_w(2 * w + 1)
            load_agg(2 * w + 1)

        ident = const.tile([P, P], F32, name="ident")
        make_identity(nc, ident[:])
        zero1 = const.tile([P, 1], F32, name="zero1")
        nc.vector.memset(zero1[:], 0.0)
        warm = const.tile([P, 1], F32, name="warm")
        nc.scalar.activation(out=warm[:], in_=zero1[:], func=ACT.Sigmoid)
        bf32 = const.tile([P, P], F32, name="bf32")
        nc.vector.memset(bf32[:], 0.0)
        nc.vector.tensor_copy(out=bf32[0:64, :], in_=braw[0:64, :])
        bias_sb = const.tile([P, 64], F32, name="bias_sb")

        def agg_t(r, h):
            xt = pst.tile([P, 512], F32, name="xt", tag="tp")
            words = araw[r][:].bitcast(F32)
            for u in range(2):
                for a in range(2):
                    nt = 2 * h + a
                    nc.tensor.transpose(
                        xt[:, 256 * u + 128 * a : 256 * u + 128 * a + 128],
                        words[:, 256 * nt + 128 * u : 256 * nt + 128 * u + 128],
                        ident[:],
                    )
            xts[(r, h)] = xt

        def agg_copy(r, h):
            if h == 0:
                agt[r] = agp.tile([P, 1024], F32, name="ag", tag="ag", align_bytes=64)
            nc.scalar.copy(
                out=agt[r][:, 512 * h : 512 * h + 512].rearrange("p (n u) -> p n u", u=2),
                in_=xts[(r, h)][:].rearrange("p (u n) -> p n u", u=2),
            )

        def agg_q(r):
            aqt[r] = aqp.tile([P, 512], U32, name="aq", tag="aq", align_bytes=64)
            ast[r] = aqp.tile([P, 512], U8, name="asc", tag="asc", align_bytes=64)
            nc.vector.quantize_mx(
                out=aqt[r][:].bitcast(FP8X4), scales=ast[r][:], in_=agt[r][:].bitcast(BF16)
            )

        def regroup(t_idx, c0, c1, on_vector):
            if t_idx not in wgt:
                wgt[t_idx] = wgp.tile([P, 1024, 4], BF16, name="wg", tag="wg", align_bytes=64)
            dst = wgt[t_idx][:, c0:c1, :].rearrange("p (c i) t -> p c t i", i=4)
            src = wraw[t_idx][:, :, c0:c1].rearrange("p t (c i) -> p c t i", i=4)
            if on_vector:
                nc.vector.tensor_copy(out=dst, in_=src)
            else:
                nc.scalar.copy(out=dst, in_=src)

        def w_q(t_idx):
            wqt[t_idx] = wqp.tile([P, 1024], U32, name="wq", tag="wq", align_bytes=64)
            wst[t_idx] = wqp.tile([P, 1024], U8, name="wsc", tag="wsc", align_bytes=64)
            nc.vector.quantize_mx(
                out=wqt[t_idx][:].bitcast(FP8X4),
                scales=wst[t_idx][:],
                in_=wgt[t_idx][:].rearrange("p c t -> p (c t)"),
            )

        def unit(uu):
            r, u = divmod(uu, 8)
            f, cb = divmod(u, 4)
            return r, f, cb, 2 * (r // 2) + f

        def one_pass(acc, t_idx, j, r):
            nc.tensor.matmul_mx(
                out=acc[:],
                lhsT=wqt[t_idx][:, 128 * j : 128 * j + 128].bitcast(FP8X4),
                lhsT_scale=wst[t_idx][:, 128 * j : 128 * j + 128],
                rhs=aqt[r][:].bitcast(FP8X4),
                rhs_scale=ast[r][:],
                start=True,
                stop=True,
            )

        def mx(uu):
            r, f, cb, t_idx = unit(uu)
            lbs[uu] = psm.tile([P, 512], F32, name="lb", tag="mx")
            one_pass(lbs[uu], t_idx, cb, r)
            rbs[uu] = psm.tile([P, 512], F32, name="rb", tag="mx")
            one_pass(rbs[uu], t_idx, 4 + cb, r)

        def sig(uu):
            r, f, cb, t_idx = unit(uu)
            col = 8 * t_idx + 4 + cb
            sts[uu] = sp.tile([P, 512], F32, name="s", tag="s")
            nc.scalar.activation(
                out=sts[uu][:], in_=rbs[uu][:], func=ACT.Sigmoid, bias=bias_sb[:, col : col + 1], scale=1.0
            )

        def stt(uu):
            r, f, cb, t_idx = unit(uu)
            col = 8 * t_idx + cb
            if f == 0:
                if cb == 0:
                    g0t[r] = g0p.tile([P, 4, 512], F32, name="g0", tag="g0")
                dst = g0t[r][:, cb, :]
            else:
                g1t[(r, cb)] = g1p.tile([P, 512], F32, name="g1", tag="g1")
                dst = g1t[(r, cb)][:]
            nc.vector.scalar_tensor_tensor(
                out=dst,
                in0=lbs[uu][:],
                scalar=bias_sb[:, col : col + 1],
                in1=sts[uu][:],
                op0=ALU.add,
                op1=ALU.mult,
            )

        def vmax(r, cb):
            nc.vector.tensor_tensor(
                out=g0t[r][:, cb, :], in0=g0t[r][:, cb, :], in1=g1t[(r, cb)][:], op=ALU.max
            )

        def out_t(r, nt, big):
            if big:
                ob = psm.tile([P, 512], F32, name="ob2", tag="mx")
            else:
                ob = pst.tile([P, 512], F32, name="ob", tag="tp")
            for cb in range(4):
                nc.tensor.transpose(
                    ob[:, 128 * cb : 128 * cb + 128], g0t[r][:, cb, 128 * nt : 128 * nt + 128], ident[:]
                )
            obs[(r, nt)] = ob

        def out_copy(r, nt, on_vector):
            if nt == 0:
                ots[r] = op.tile([P, 4, 512], F32, name="o", tag="o")
            if on_vector:
                nc.vector.tensor_copy(out=ots[r][:, nt, :], in_=obs[(r, nt)][:])
            else:
                nc.scalar.copy(out=ots[r][:, nt, :], in_=obs[(r, nt)][:])

        def store(r, n0, n1):
            w, i = divmod(r, 2)
            nc.sync.dma_start(
                out=out[i, w].rearrange("(p nt) c -> p nt c", nt=4)[:, n0:n1, :], in_=ots[r][:, n0:n1, :]
            )

        hv = CV // 2
        hs = (1024 - CV) // 2

        agg_t(0, 0)
        agg_t(0, 1)
        bt = psm.tile([P, 512], F32, name="bt", tag="mx")
        nc.tensor.transpose(bt[:, 0:128], bf32[:], ident[:])
        nc.vector.tensor_copy(out=bias_sb[:], in_=bt[:, 0:64])
        agg_copy(0, 0)
        agg_copy(0, 1)
        regroup(0, 0, CV, True)
        regroup(0, CV, 1024, False)
        agg_q(0)
        w_q(0)
        regroup(1, 0, CV, True)
        regroup(1, CV, 1024, False)
        mx(0)
        mx(1)

        for r in range(N_ROUNDS):
            for u in range(8):
                uu = 8 * r + u
                if uu + 2 < 8 * N_ROUNDS:
                    mx(uu + 2)
                if u == 0 and r + 1 < N_ROUNDS:
                    agg_t(r + 1, 0)
                    agg_t(r + 1, 1)
                if r >= 1:
                    if u == 3:
                        out_t(r - 1, 0, False)
                        out_t(r - 1, 1, False)
                    if u == 5:
                        out_t(r - 1, 2, False)
                    if u == 6:
                        out_t(r - 1, 3, False)
                sig(uu)
                if u == 0 and r + 2 < 8:
                    regroup(r + 2, CV, CV + hs, False)
                if u in (1, 2) and r + 1 < N_ROUNDS:
                    agg_copy(r + 1, u - 1)
                if u == 3 and r + 2 < 8:
                    regroup(r + 2, CV + hs, 1024, False)
                if u >= 4 and r >= 1:
                    out_copy(r - 1, u - 4, False)
                    if u == 7:
                        store(r - 1, 0, 4)
                stt(uu)
                if u == 0 and r + 1 < 8:
                    w_q(r + 1)
                if u == 1 and r >= 1:
                    vmax(r - 1, 3)
                if u == 2 and r + 2 < 8:
                    regroup(r + 2, 0, hv, True)
                if u == 3 and r + 2 < 8:
                    regroup(r + 2, hv, CV, True)
                if u == 4 and r + 1 < N_ROUNDS:
                    agg_q(r + 1)
                if u >= 5:
                    vmax(r, u - 5)

        last = N_ROUNDS - 1
        vmax(last, 3)
        out_t(last, 0, False)
        out_t(last, 1, False)
        out_t(last, 2, True)
        out_t(last, 3, True)
        out_copy(last, 0, False)
        out_copy(last, 1, True)
        store(last, 0, 2)
        out_copy(last, 2, False)
        out_copy(last, 3, True)
        store(last, 2, 4)
